import numpy as np
import ml_dtypes


def mxq(x, axis, fmt="e4m3"):
    dtype, down = {"e4m3": (ml_dtypes.float8_e4m3fn, 7), "e5m2": (ml_dtypes.float8_e5m2, 14)}[fmt]
    v = np.moveaxis(np.asarray(x, np.float32).astype(ml_dtypes.bfloat16).astype(np.float64), axis, -1)
    blocks = v.reshape(v.shape[:-1] + (-1, 32))
    amax = np.abs(blocks).max(-1, keepdims=True)
    byte = np.maximum(np.where(amax > 0, np.frexp(amax)[1] - 1 + 127, 0) - down, 1)
    scale = np.exp2(byte - 127.0)
    codes = (blocks / scale).astype(np.float32).astype(dtype).astype(np.float64)
    return np.moveaxis((codes * scale).reshape(v.shape), -1, axis)


WIDE = False


def mx_kscale(k):
    if not WIDE:
        return np.ones(k)
    levels = np.array([18, -18])
    if k % 512:
        return np.exp2(np.random.permutation(np.resize(levels, k // 32))).repeat(32)
    a = np.empty((k // 512, 16))
    for p in range(k // 512):
        a[p, :8] = np.random.permutation(np.resize(levels, 8))
        for g in range(8):
            far = levels[np.abs(levels - a[p, g]) >= 10]
            a[p, g + 8] = far[np.random.randint(len(far))]
    return np.exp2(a.ravel()).repeat(32)


BF16 = ml_dtypes.bfloat16


def bf(x):
    return np.asarray(x, np.float32).astype(BF16)


def f64(x):
    return np.asarray(x).astype(np.float64)


BS, BLOCK, HID, G = 512, 512, 1024, 4


def elu_grad(v):
    return np.where(v > 0.0, 1.0, np.exp(np.minimum(v, 0.0)))


def to_blocks(a):
    return a.reshape(a.shape[0], -1, BLOCK).transpose(1, 0, 2)


def setup_inputs():
    s = mx_kscale(BS)
    u = mx_kscale(BLOCK)
    u = u / u.max()
    v = mx_kscale(HID)
    x0 = bf(np.random.standard_normal((BS, G * BLOCK)))
    w1_0 = bf(np.random.standard_normal((G, BLOCK, HID)) / np.sqrt(BLOCK))
    b1 = bf(np.random.standard_normal((G, 1, HID)) * 0.2)
    w2_0 = bf(np.random.standard_normal((G, HID, BLOCK)) / np.sqrt(HID))
    b2 = bf(np.random.standard_normal((G, 1, BLOCK)) * 0.2)
    g = np.random.standard_normal((BS, G, BLOCK)) * np.exp2(np.random.randint(-6, 1, (BS, 1, 1))) * 4.0
    g = bf((g / s[:, None, None] * u[None, None, :]).reshape(BS, G * BLOCK))
    z1 = to_blocks(f64(x0)) @ f64(w1_0) + f64(b1)
    return {"x_blocks": bf(f64(x0) * s[:, None]),
            "w1": bf(f64(w1_0) / v[None, None, :]),
            "b1": b1,
            "w2": bf(f64(w2_0) * v[None, :, None] / u[None, None, :]),
            "b2": b2,
            "z1": np.asarray(z1, np.float32),
            "grad_out": g}


def reference(x_blocks, w1, b1, w2, b2, z1, grad_out):
    bs = x_blocks.shape[0]
    z = to_blocks(f64(x_blocks))
    g = to_blocks(f64(grad_out))
    dh = mxq(g, 2, "e5m2") @ mxq(f64(w2), 2, "e4m3").transpose(0, 2, 1)
    dz1 = dh * elu_grad(f64(z1))
    dz = mxq(dz1, 2, "e5m2") @ mxq(f64(w1), 2, "e4m3").transpose(0, 2, 1)
    dz = dz + g
    dx = dz.transpose(1, 0, 2).reshape(bs, -1)
    dw1 = mxq(z, 1, "e4m3").transpose(0, 2, 1) @ mxq(dz1, 1, "e5m2")
    return dx, dw1

@@ -1,0 +1,303 @@
+from contextlib import ExitStack
+
+import concourse.mybir as mybir
+from concourse.masks import make_identity
+
+TOKENS, D_BLOCK, HID, BLOCKS = 512, 512, 1024, 4
+FLOPS = 3 * 2 * BLOCKS * TOKENS * D_BLOCK * HID
+BYTES = 2 * (2 * TOKENS * BLOCKS * D_BLOCK + 2 * BLOCKS * D_BLOCK * HID) + 4 * (
+    BLOCKS * TOKENS * HID + TOKENS * BLOCKS * D_BLOCK + BLOCKS * D_BLOCK * HID
+)
+
+F32 = mybir.dt.float32
+BF16 = mybir.dt.bfloat16
+U32 = mybir.dt.uint32
+U8 = mybir.dt.uint8
+E4M3 = mybir.dt.float8_e4m3fn_x4
+E5M2 = mybir.dt.float8_e5m2_x4
+ACT = mybir.ActivationFunctionType
+ALU = mybir.AluOpType
+
+P = 128
+N = 512
+R = 4
+
+
+def tile_blockresmlp_mixerblock_pb_v_kernel(tc, x_blocks, w1, b1, w2, b2, z1, grad_out, out_0, out_1):
+    nc = tc.nc
+
+    g_view = grad_out.rearrange("(p j) c -> p j c", j=R)
+    x_view = x_blocks.rearrange("(p j) c -> p j c", j=R)
+    dx_view = out_0.rearrange("(p j) c -> p j c", j=R)
+
+    with ExitStack() as ctx:
+        const = ctx.enter_context(tc.tile_pool(name="const", bufs=1))
+        raw = ctx.enter_context(tc.tile_pool(name="raw", bufs=2))
+        work = ctx.enter_context(tc.tile_pool(name="work", bufs=2))
+        codes = ctx.enter_context(tc.tile_pool(name="codes", bufs=2))
+        outs = ctx.enter_context(tc.tile_pool(name="outs", bufs=3))
+        psum = ctx.enter_context(tc.psum_pool(name="psum", bufs=8))
+
+        ident = const.tile([P, P], F32, name="ident")
+        make_identity(nc, ident[:])
+        warm = const.tile([P, 1], F32, name="warm")
+        nc.vector.memset(warm[:], 0.0)
+        nc.scalar.activation(warm[:], warm[:], ACT.Exp)
+
+        ctx.enter_context(tc.manual_schedule())
+
+        t_g, t_x, t_w2, t_w1, t_z = {}, {}, {}, {}, {}
+        q_g, q_x, q_w2, q_w1, q_dz, q_dzt = {}, {}, {}, {}, {}, {}
+        t_gg, t_xi, t_w2g, t_w1g, t_f, t_di, t_d = {}, {}, {}, {}, {}, {}, {}
+        t_ow, t_dx = {}, {}
+
+        def load_g(n):
+            t_g[n] = raw.tile([P, R, N], BF16, name="g_raw", bufs=3)
+            nc.sync.dma_start(out=t_g[n][:], in_=g_view[:, :, n * N : (n + 1) * N])
+
+        def load_x(n):
+            t_x[n] = raw.tile([P, R, N], BF16, name="x_raw", bufs=2)
+            nc.sync.dma_start(out=t_x[n][:], in_=x_view[:, :, n * N : (n + 1) * N])
+
+        def load_w2(n):
+            t_w2[n] = raw.tile([P, 2, R, N], BF16, name="w2_raw", bufs=2)
+            view = w2[n].rearrange("(g p r) d -> p g r d", g=2, r=R)
+            for gh in range(2):
+                nc.sync.dma_start(out=t_w2[n][:, gh], in_=view[:, gh])
+
+        def load_w1(n):
+            t_w1[n] = raw.tile([P, R, HID], BF16, name="w1_raw", bufs=2)
+            nc.sync.dma_start(out=t_w1[n][:], in_=w1[n].rearrange("(p r) h -> p r h", r=R))
+
+        def load_z(n):
+            t_z[n] = raw.tile([P, R, HID], F32, name="z_raw", bufs=3)
+            view = z1[n].rearrange("(p j) h -> p j h", j=R)
+            for k in range(2):
+                if n == 0:
+                    nc.sync.dma_start(out=t_z[n][:, :, k * N : (k + 1) * N], in_=view[:, :, k * N : (k + 1) * N])
+                else:
+                    nc.sync.dma_start(out=t_z[n][:, 2 * k : 2 * k + 2, :], in_=view[:, 2 * k : 2 * k + 2, :])
+
+        def copy(engine, out, in_):
+            if engine == "V":
+                nc.vector.tensor_copy(out=out, in_=in_)
+            else:
+                nc.scalar.copy(out=out, in_=in_)
+
+        def bank4(ins):
+            bank = psum.tile([P, R, P], F32, name="bank")
+            for k in range(R):
+                nc.tensor.transpose(bank[:, k, :], ins[k], ident[:])
+            return bank
+
+        def rows_bank(words, grouped, jp, engine):
+            bank = bank4([words[:, 2 * jp + e, u::2] for e in range(2) for u in range(2)])
+            copy(
+                engine,
+                grouped.bitcast(F32)[:, 2 * P * jp : 2 * P * (jp + 1), :].rearrange("q (e p) u -> q e p u", e=2),
+                bank[:].rearrange("q (e u) p -> q e p u", e=2),
+            )
+
+        def quads_bank(words, grouped, s, engine):
+            bank = bank4([words[:, 2 * s + e, u::2] for e in range(2) for u in range(2)])
+            copy(
+                engine,
+                grouped.bitcast(F32).rearrange("q (p s e) u -> q p s (e u)", s=2, e=2)[:, :, s, :],
+                bank[:].rearrange("q k p -> q p k"),
+            )
+
+        def quantize(grouped, dtype, name, bufs):
+            c = codes.tile([P, N], U32, name=name + "_c", bufs=bufs, align_bytes=64)
+            s = codes.tile([P, N], U8, name=name + "_s", bufs=bufs, align_bytes=64)
+            nc.vector.quantize_mx(
+                out=c[:].bitcast(dtype), scales=s[:], in_=grouped[:].rearrange("p c t -> p (c t)")
+            )
+            return c, s
+
+        def mx(bank, a, a_type, a_cols, b, b_type, start, stop):
+            nc.tensor.matmul_mx(
+                out=bank[:],
+                lhsT=a[0][:, a_cols].bitcast(a_type),
+                lhsT_scale=a[1][:, a_cols],
+                rhs=b[0][:].bitcast(b_type),
+                rhs_scale=b[1][:],
+                start=start,
+                stop=stop,
+            )
+
+        def grouped_tile(name, bufs):
+            return work.tile([P, N, R], BF16, name=name, bufs=bufs, align_bytes=64)
+
+        def tr_g(n, jp, engine):
+            if jp == 0:
+                t_gg[n] = grouped_tile("g_grp", 1)
+            rows_bank(t_g[n][:].bitcast(F32), t_gg[n][:], jp, engine)
+
+        def tr_w2(n, gh, s, engine):
+            if s == 0:
+                t_w2g[n, gh] = grouped_tile("w2_grp", 2)
+            quads_bank(t_w2[n][:, gh].bitcast(F32), t_w2g[n, gh][:], s, engine)
+
+        def tr_w1(n, gh, s, engine):
+            if s == 0:
+                t_w1g[n, gh] = grouped_tile("w1_grp", 2)
+            quads_bank(t_w1[n][:].bitcast(F32)[:, :, 256 * gh : 256 * (gh + 1)], t_w1g[n, gh][:], s, engine)
+
+        def tr_dz(n, gh, jp, engine):
+            if jp == 0:
+                t_f[n, gh] = grouped_tile("f_grp", 2)
+            rows_bank(t_d[n, gh][:].bitcast(F32), t_f[n, gh][:], jp, engine)
+
+        def interleave(name, src, bufs):
+            dst = grouped_tile(name, bufs)
+            nc.vector.tensor_copy(
+                out=dst[:].rearrange("p (c i) t -> p c t i", i=4), in_=src[:].rearrange("p t (c i) -> p c t i", i=4)
+            )
+            return dst
+
+        def exp(n, gh):
+            z = t_z[n][:, :, gh * N : (gh + 1) * N]
+            nc.scalar.activation(z, z, ACT.Exp)
+
+        def dh_mm(n, gh, j):
+            bank = psum.tile([P, N], F32, name="bank")
+            mx(bank, q_g[n], E5M2, slice(j * P, (j + 1) * P), q_w2[n, gh], E4M3, True, True)
+            return bank
+
+        def stt(n, gh, j, bank):
+            if j == 0:
+                t_d[n, gh] = work.tile([P, R, N], BF16, name="dz1", bufs=3, align_bytes=64)
+            nc.vector.scalar_tensor_tensor(
+                out=t_d[n, gh][:, j, :],
+                in0=t_z[n][:, j, gh * N : (gh + 1) * N],
+                scalar=1.0,
+                in1=bank[:],
+                op0=ALU.min,
+                op1=ALU.mult,
+            )
+
+        def dx_mm(n, j):
+            bank = psum.tile([P, N], F32, name="bank")
+            for gh in range(2):
+                mx(bank, q_dzt[n, gh], E5M2, slice(j * P, (j + 1) * P), q_w1[n, gh], E4M3, gh == 0, gh == 1)
+            return bank
+
+        def dx_add(n, j, bank):
+            if j % 2 == 0:
+                t_dx[n, j // 2] = outs.tile([P, 2, N], F32, name="dx", bufs=3)
+            t = t_dx[n, j // 2]
+            nc.vector.tensor_tensor(out=t[:, j % 2, :], in0=bank[:], in1=t_g[n][:, j, :], op=ALU.add)
+            if j % 2 == 1:
+                nc.sync.dma_start(out=dx_view[:, j - 1 : j + 1, n * N : (n + 1) * N], in_=t[:])
+
+        def dw_mm(n, dd, gh):
+            bank = psum.tile([P, N], F32, name="bank")
+            mx(bank, q_x[n], E4M3, slice(dd * P, (dd + 1) * P), q_dz[n, gh], E5M2, True, True)
+            return bank
+
+        def dw_out(n, dd, gh, bank, engine):
+            if (n, dd) not in t_ow:
+                t_ow[n, dd] = outs.tile([P, 2, N], F32, name="dw", bufs=5)
+            t = t_ow[n, dd]
+            copy(engine, t[:, gh, :], bank[:])
+            if gh == 1:
+                nc.sync.dma_start(
+                    out=out_1[n, dd * P : (dd + 1) * P, :], in_=t[:].rearrange("p g h -> p (g h)")
+                )
+
+        load_g(0)
+        load_w2(0)
+        load_z(0)
+        load_w1(0)
+        load_x(0)
+        load_g(1)
+        load_w2(1)
+        load_z(1)
+        load_w1(1)
+        load_x(1)
+
+        tr_g(0, 0, "V")
+        tr_g(0, 1, "S")
+        tr_w2(0, 0, 0, "V")
+        tr_w2(0, 0, 1, "S")
+        q_g[0] = quantize(t_gg[0], E5M2, "g", 2)
+        tr_w2(0, 1, 0, "V")
+        tr_w2(0, 1, 1, "S")
+        q_w2[0, 0] = quantize(t_w2g[0, 0], E4M3, "w2", 4)
+        exp(0, 0)
+        q_w2[0, 1] = quantize(t_w2g[0, 1], E4M3, "w2", 4)
+        exp(0, 1)
+
+        for n in range(BLOCKS):
+            last = n == BLOCKS - 1
+            if n + 2 < BLOCKS:
+                load_g(n + 2)
+                load_w2(n + 2)
+                load_z(n + 2)
+            dws = [(dd, gh) for dd in range(4) for gh in range(2)]
+
+            def dw_pair(k):
+                if n > 0:
+                    pair = dws[2 * k : 2 * k + 2]
+                    bs = [dw_mm(n - 1, dd, gh) for dd, gh in pair]
+                    for (dd, gh), b in zip(pair, bs):
+                        dw_out(n - 1, dd, gh, b, "S")
+
+            for gh in range(2):
+                for h in range(2):
+                    bs = [dh_mm(n, gh, 2 * h + e) for e in range(2)]
+                    for e in range(2):
+                        stt(n, gh, 2 * h + e, bs[e])
+                    dw_pair(2 * gh + h)
+                if gh == 1:
+                    tr_dz(n, 0, 0, "S")
+                    tr_dz(n, 0, 1, "S")
+            t_di[n, 0] = interleave("dz_grp", t_d[n, 0], 2)
+            tr_dz(n, 1, 0, "S")
+            tr_dz(n, 1, 1, "S")
+            t_di[n, 1] = interleave("dz_grp", t_d[n, 1], 2)
+            q_dz[n, 0] = quantize(t_di[n, 0], E5M2, "dz", 4)
+            q_dzt[n, 0] = quantize(t_f[n, 0], E5M2, "dzt", 2)
+            q_dz[n, 1] = quantize(t_di[n, 1], E5M2, "dz", 4)
+            t_xi[n] = interleave("x_grp", t_x[n], 1)
+            q_dzt[n, 1] = quantize(t_f[n, 1], E5M2, "dzt", 2)
+            if n + 2 < BLOCKS:
+                load_w1(n + 2)
+                load_x(n + 2)
+            if n == 0:
+                for gh in range(2):
+                    tr_w1(0, gh, 0, "S")
+                    tr_w1(0, gh, 1, "S")
+            if not last:
+                tr_g(n + 1, 0, "S")
+                tr_g(n + 1, 1, "S")
+                for gh in range(2):
+                    tr_w2(n + 1, gh, 0, "S")
+                    tr_w2(n + 1, gh, 1, "S")
+            if n == 0:
+                for gh in range(2):
+                    q_w1[0, gh] = quantize(t_w1g[0, gh], E4M3, "w1", 4)
+            q_x[n] = quantize(t_xi[n], E4M3, "x", 2)
+            dxb = [dx_mm(n, j) for j in range(2)]
+            if not last:
+                q_g[n + 1] = quantize(t_gg[n + 1], E5M2, "g", 2)
+            for j in range(2):
+                dx_add(n, j, dxb[j])
+            dxb = [dx_mm(n, j) for j in range(2, 4)]
+            if not last:
+                for gh in range(2):
+                    q_w2[n + 1, gh] = quantize(t_w2g[n + 1, gh], E4M3, "w2", 4)
+            for j in range(2, 4):
+                dx_add(n, j, dxb[j - 2])
+            if not last:
+                for gh in range(2):
+                    tr_w1(n + 1, gh, 0, "S")
+                    tr_w1(n + 1, gh, 1, "S")
+                    exp(n + 1, gh)
+                for gh in range(2):
+                    q_w1[n + 1, gh] = quantize(t_w1g[n + 1, gh], E4M3, "w1", 4)
+        n = BLOCKS - 1
+        for gh in range(2):
+            for dd in range(4):
+                b = dw_mm(n, dd, gh)
+                dw_out(n, dd, gh, b, "S" if (dd + gh) % 2 == 0 else "V")

@@ -21,6 +21,31 @@ ALU = mybir.AluOpType
 P = 128
 N = 512
 R = 4
+BUFS = {"w1": 2, "z": 2, "E": 2, "grp": 7, "dz1": 2, "dx": 3, "dw": 6}
+PLAN = [
+    (0, "lg"),
+    (0, "lw"),
+    (0, "lz"),
+    (0, "lv"),
+    (1, "lw"),
+    (0, "lx"),
+    (1, "lg"),
+    (1, "lz"),
+    (2, "lw"),
+    (1, "lv"),
+    (3, "lw"),
+    (2, "lz"),
+    (3, "lv"),
+    (1, "lx"),
+    (3, "lz"),
+    (2, "lv"),
+    (0, "tg:SS qg tw20:VS exp0 qw20 tw21:VV qw21 exp1 dh0 dh1"),
+    (0, "stt0 stt1 tdz0:SS tw11:SS tdz1:VS di1:s qdzt0 di0:G qdz0 qw11 qdzt1 tw10:SV qdz1 qw10 intx:V tw20+:SS tw21+:SS qx qw21+ dxp0 dwp0:SV dwp1:SV qw20+ tg+:SS qg+ dxp1 dh0+ exp0+ exp1+ dh1+"),
+    (1, "intx:G tw20+:SS stt0 stt1 dxp1- tg+:VS di0:G tdz0:SV di1:V qw20+ qg+ tdz1:SS qdzt1 tw10:SS dwp0-:SSSSSV qdzt0 dxp0- tw11:SS dwp1-:SSSV tw21+:SS exp0+ qw10 qdz1 qdz0 exp1+ qw11 qw21+ dh0+ dh1+ qx"),
+    (2, "intx:G tw20+:SS stt0 stt1 dxp1- tg+:VS di0:G tdz0:SV di1:V qw20+ qg+ tdz1:SS qdzt1 tw10:SS dwp0-:SSSSSV qdzt0 dxp0- tw11:SS dwp1-:SSSV tw21+:SS exp0+ qw10 qdz1 qdz0 exp1+ qw11 qw21+ dh0+ dh1+ qx"),
+    (3, "tw11:SS stt0 stt1 dxp0- tw10:VS intx:G dwp1-:SV di0:G dwp0-:SSSV tdz1:SS di1:G tdz0:SS qdz0 qx dxp1- qdz1 qw11 qdzt0 qdzt1 qw10"),
+    (4, "dwg0-:SSSV dwg1-:SSV dxp1- dxp0-"),
+]
 
 
 def tile_blockresmlp_mixerblock_pb_v_kernel(tc, x_blocks, w1, b1, w2, b2, z1, grad_out, out_0, out_1):
@@ -46,18 +71,30 @@ def tile_blockresmlp_mixerblock_pb_v_kernel(tc, x_blocks, w1, b1, w2, b2, z1, gr
 
         ctx.enter_context(tc.manual_schedule())
 
-        t_g, t_x, t_w2, t_w1, t_z = {}, {}, {}, {}, {}
+        t_g, t_x, t_w2, t_w1, t_z, t_e = {}, {}, {}, {}, {}, {}
         q_g, q_x, q_w2, q_w1, q_dz, q_dzt = {}, {}, {}, {}, {}, {}
         t_gg, t_xi, t_w2g, t_w1g, t_f, t_di, t_d = {}, {}, {}, {}, {}, {}, {}
         t_ow, t_dx = {}, {}
+        done = set()
 
         def load_g(n):
-            t_g[n] = raw.tile([P, R, N], BF16, name="g_raw", bufs=3)
-            nc.sync.dma_start(out=t_g[n][:], in_=g_view[:, :, n * N : (n + 1) * N])
+            if n == 0:
+                first = raw.tile([P, R, N], BF16, name="g_first", bufs=1)
+                nc.sync.dma_start(out=first[:], in_=g_view[:, :, 0:N])
+                t_g[0] = first[:]
+            elif n == 1:
+                rest = raw.tile([P, R, 3 * N], BF16, name="g_rest", bufs=1)
+                nc.sync.dma_start(out=rest[:], in_=g_view[:, :, N : 4 * N])
+                for m in range(1, 4):
+                    t_g[m] = rest[:, :, (m - 1) * N : m * N]
 
         def load_x(n):
-            t_x[n] = raw.tile([P, R, N], BF16, name="x_raw", bufs=2)
-            nc.sync.dma_start(out=t_x[n][:], in_=x_view[:, :, n * N : (n + 1) * N])
+            if n > 0:
+                return
+            whole = raw.tile([P, R, BLOCKS * N], BF16, name="x_raw", bufs=1)
+            nc.sync.dma_start(out=whole[:], in_=x_view)
+            for m in range(BLOCKS):
+                t_x[m] = whole[:, :, m * N : (m + 1) * N]
 
         def load_w2(n):
             t_w2[n] = raw.tile([P, 2, R, N], BF16, name="w2_raw", bufs=2)
@@ -66,17 +103,21 @@ def tile_blockresmlp_mixerblock_pb_v_kernel(tc, x_blocks, w1, b1, w2, b2, z1, gr
                 nc.sync.dma_start(out=t_w2[n][:, gh], in_=view[:, gh])
 
         def load_w1(n):
-            t_w1[n] = raw.tile([P, R, HID], BF16, name="w1_raw", bufs=2)
+            t_w1[n] = raw.tile([P, R, HID], BF16, name="w1_raw", bufs=BUFS["w1"])
             nc.sync.dma_start(out=t_w1[n][:], in_=w1[n].rearrange("(p r) h -> p r h", r=R))
 
         def load_z(n):
-            t_z[n] = raw.tile([P, R, HID], F32, name="z_raw", bufs=3)
+            t_z[n] = raw.tile([P, R, HID], F32, name="z_raw", bufs=BUFS["z"])
             view = z1[n].rearrange("(p j) h -> p j h", j=R)
-            for k in range(2):
-                if n == 0:
-                    nc.sync.dma_start(out=t_z[n][:, :, k * N : (k + 1) * N], in_=view[:, :, k * N : (k + 1) * N])
-                else:
-                    nc.sync.dma_start(out=t_z[n][:, 2 * k : 2 * k + 2, :], in_=view[:, 2 * k : 2 * k + 2, :])
+            if n == 0:
+                for k in range(2):
+                    for jp in range(2):
+                        js, hs = slice(2 * jp, 2 * jp + 2), slice(k * N, (k + 1) * N)
+                        nc.sync.dma_start(out=t_z[n][:, js, hs], in_=view[:, js, hs])
+            else:
+                for jp in range(2):
+                    js = slice(2 * jp, 2 * jp + 2)
+                    nc.sync.dma_start(out=t_z[n][:, js, :], in_=view[:, js, :])
 
         def copy(engine, out, in_):
             if engine == "V":
@@ -90,20 +131,18 @@ def tile_blockresmlp_mixerblock_pb_v_kernel(tc, x_blocks, w1, b1, w2, b2, z1, gr
                 nc.tensor.transpose(bank[:, k, :], ins[k], ident[:])
             return bank
 
-        def rows_bank(words, grouped, jp, engine):
-            bank = bank4([words[:, 2 * jp + e, u::2] for e in range(2) for u in range(2)])
+        def rows_bank(ins, grouped, half, engine):
             copy(
                 engine,
-                grouped.bitcast(F32)[:, 2 * P * jp : 2 * P * (jp + 1), :].rearrange("q (e p) u -> q e p u", e=2),
-                bank[:].rearrange("q (e u) p -> q e p u", e=2),
+                grouped.bitcast(F32)[:, 2 * P * half : 2 * P * (half + 1), :].rearrange("q (e p) u -> q e p u", e=2),
+                bank4(ins)[:].rearrange("q (e u) p -> q e p u", e=2),
             )
 
-        def quads_bank(words, grouped, s, engine):
-            bank = bank4([words[:, 2 * s + e, u::2] for e in range(2) for u in range(2)])
+        def pairs_bank(ins, grouped, half, engine):
             copy(
                 engine,
-                grouped.bitcast(F32).rearrange("q (p s e) u -> q p s (e u)", s=2, e=2)[:, :, s, :],
-                bank[:].rearrange("q k p -> q p k"),
+                grouped.bitcast(F32)[:, 2 * P * half : 2 * P * (half + 1), :].rearrange("q (p e) u -> q p (e u)", e=2),
+                bank4(ins)[:].rearrange("q k p -> q p k"),
             )
 
         def quantize(grouped, dtype, name, bufs):
@@ -130,34 +169,67 @@ def tile_blockresmlp_mixerblock_pb_v_kernel(tc, x_blocks, w1, b1, w2, b2, z1, gr
 
         def tr_g(n, jp, engine):
             if jp == 0:
-                t_gg[n] = grouped_tile("g_grp", 1)
-            rows_bank(t_g[n][:].bitcast(F32), t_gg[n][:], jp, engine)
+                t_gg[n] = grouped_tile("grp", BUFS["grp"])
+            words = t_g[n].bitcast(F32)
+            rows_bank([words[:, 2 * jp + e, u::2] for e in range(2) for u in range(2)], t_gg[n][:], jp, engine)
 
         def tr_w2(n, gh, s, engine):
             if s == 0:
-                t_w2g[n, gh] = grouped_tile("w2_grp", 2)
-            quads_bank(t_w2[n][:, gh].bitcast(F32), t_w2g[n, gh][:], s, engine)
+                t_w2g[n, gh] = grouped_tile("grp", BUFS["grp"])
+            words = t_w2[n][:, gh].bitcast(F32)
+            pairs_bank([words[:, 2 * s + e, u::2] for e in range(2) for u in range(2)], t_w2g[n, gh][:], s, engine)
 
         def tr_w1(n, gh, s, engine):
             if s == 0:
-                t_w1g[n, gh] = grouped_tile("w1_grp", 2)
-            quads_bank(t_w1[n][:].bitcast(F32)[:, :, 256 * gh : 256 * (gh + 1)], t_w1g[n, gh][:], s, engine)
+                t_w1g[n, gh] = grouped_tile("grp", BUFS["grp"])
+            words = t_w1[n][:].bitcast(F32)
+            pairs_bank(
+                [words[:, 2 * s + e, 256 * gh + u : 256 * (gh + 1) : 2] for e in range(2) for u in range(2)],
+                t_w1g[n, gh][:],
+                s,
+                engine,
+            )
 
         def tr_dz(n, gh, jp, engine):
             if jp == 0:
-                t_f[n, gh] = grouped_tile("f_grp", 2)
-            rows_bank(t_d[n, gh][:].bitcast(F32), t_f[n, gh][:], jp, engine)
-
-        def interleave(name, src, bufs):
-            dst = grouped_tile(name, bufs)
-            nc.vector.tensor_copy(
-                out=dst[:].rearrange("p (c i) t -> p c t i", i=4), in_=src[:].rearrange("p t (c i) -> p c t i", i=4)
+                t_f[n, gh] = grouped_tile("grp", BUFS["grp"])
+            words = t_d[n, gh][:].bitcast(F32)
+            rows_bank(
+                [words[:, 2 * jp + e, P * u : P * (u + 1)] for e in range(2) for u in range(2)],
+                t_f[n, gh][:],
+                jp,
+                engine,
             )
+
+        def interleave(name, src, bufs, engine):
+            dst = grouped_tile(name, bufs)
+            if engine == "G":
+                nc.gpsimd.tensor_scalar(
+                    out=dst[:],
+                    in0=src.rearrange("p t c -> p c t"),
+                    scalar1=1.0,
+                    scalar2=0.0,
+                    op0=ALU.mult,
+                    op1=ALU.add,
+                )
+            elif engine == "s":
+                nc.scalar.copy(
+                    out=dst[:].rearrange("p (c i) t -> p c t i", i=4), in_=src.rearrange("p t (c i) -> p c t i", i=4)
+                )
+            else:
+                nc.vector.tensor_copy(
+                    out=dst[:].rearrange("p (c i) t -> p c t i", i=4), in_=src.rearrange("p t (c i) -> p c t i", i=4)
+                )
             return dst
 
         def exp(n, gh):
-            z = t_z[n][:, :, gh * N : (gh + 1) * N]
-            nc.scalar.activation(z, z, ACT.Exp)
+            t_e[n, gh] = work.tile([P, R, N], F32, name="e", bufs=BUFS["E"])
+            for j in range(R):
+                nc.scalar.activation(
+                    t_e[n, gh][:, j, :].rearrange("p (s i e) -> p s i e", s=2, e=2),
+                    t_z[n][:, j, gh * N : (gh + 1) * N].rearrange("p (i s e) -> p s i e", s=2, e=2),
+                    ACT.Exp,
+                )
 
         def dh_mm(n, gh, j):
             bank = psum.tile([P, N], F32, name="bank")
@@ -166,10 +238,10 @@ def tile_blockresmlp_mixerblock_pb_v_kernel(tc, x_blocks, w1, b1, w2, b2, z1, gr
 
         def stt(n, gh, j, bank):
             if j == 0:
-                t_d[n, gh] = work.tile([P, R, N], BF16, name="dz1", bufs=3, align_bytes=64)
+                t_d[n, gh] = work.tile([P, R, N], BF16, name="dz1", bufs=BUFS["dz1"], align_bytes=64)
             nc.vector.scalar_tensor_tensor(
                 out=t_d[n, gh][:, j, :],
-                in0=t_z[n][:, j, gh * N : (gh + 1) * N],
+                in0=t_e[n, gh][:, j, :],
                 scalar=1.0,
                 in1=bank[:],
                 op0=ALU.min,
@@ -184,9 +256,14 @@ def tile_blockresmlp_mixerblock_pb_v_kernel(tc, x_blocks, w1, b1, w2, b2, z1, gr
 
         def dx_add(n, j, bank):
             if j % 2 == 0:
-                t_dx[n, j // 2] = outs.tile([P, 2, N], F32, name="dx", bufs=3)
+                t_dx[n, j // 2] = outs.tile([P, 2, N], F32, name="dx", bufs=BUFS["dx"])
             t = t_dx[n, j // 2]
-            nc.vector.tensor_tensor(out=t[:, j % 2, :], in0=bank[:], in1=t_g[n][:, j, :], op=ALU.add)
+            nc.vector.tensor_tensor(
+                out=t[:, j % 2, :].rearrange("p (i s e) -> p i s e", s=2, e=2),
+                in0=bank[:].rearrange("p (s i e) -> p i s e", s=2, e=2),
+                in1=t_g[n][:, j, :].rearrange("p (i s e) -> p i s e", s=2, e=2),
+                op=ALU.add,
+            )
             if j % 2 == 1:
                 nc.sync.dma_start(out=dx_view[:, j - 1 : j + 1, n * N : (n + 1) * N], in_=t[:])
 
@@ -196,108 +273,89 @@ def tile_blockresmlp_mixerblock_pb_v_kernel(tc, x_blocks, w1, b1, w2, b2, z1, gr
             return bank
 
         def dw_out(n, dd, gh, bank, engine):
-            if (n, dd) not in t_ow:
-                t_ow[n, dd] = outs.tile([P, 2, N], F32, name="dw", bufs=5)
+            first = (n, dd) not in t_ow
+            if first:
+                t_ow[n, dd] = outs.tile([P, 2, N], F32, name="dw", bufs=BUFS["dw"])
             t = t_ow[n, dd]
-            copy(engine, t[:, gh, :], bank[:])
-            if gh == 1:
-                nc.sync.dma_start(
-                    out=out_1[n, dd * P : (dd + 1) * P, :], in_=t[:].rearrange("p g h -> p (g h)")
-                )
+            copy(
+                engine,
+                t[:, gh, :].rearrange("p (i s e) -> p i s e", s=2, e=2),
+                bank[:].rearrange("p (s i e) -> p i s e", s=2, e=2),
+            )
+            if not first:
+                nc.sync.dma_start(out=out_1[n, dd * P : (dd + 1) * P, :], in_=t[:].rearrange("p g h -> p (g h)"))
 
-        load_g(0)
-        load_w2(0)
-        load_z(0)
-        load_w1(0)
-        load_x(0)
-        load_g(1)
-        load_w2(1)
-        load_z(1)
-        load_w1(1)
-        load_x(1)
+        pend = {}
 
-        tr_g(0, 0, "V")
-        tr_g(0, 1, "S")
-        tr_w2(0, 0, 0, "V")
-        tr_w2(0, 0, 1, "S")
-        q_g[0] = quantize(t_gg[0], E5M2, "g", 2)
-        tr_w2(0, 1, 0, "V")
-        tr_w2(0, 1, 1, "S")
-        q_w2[0, 0] = quantize(t_w2g[0, 0], E4M3, "w2", 4)
-        exp(0, 0)
-        q_w2[0, 1] = quantize(t_w2g[0, 1], E4M3, "w2", 4)
-        exp(0, 1)
-
-        for n in range(BLOCKS):
-            last = n == BLOCKS - 1
-            if n + 2 < BLOCKS:
-                load_g(n + 2)
-                load_w2(n + 2)
-                load_z(n + 2)
-            dws = [(dd, gh) for dd in range(4) for gh in range(2)]
-
-            def dw_pair(k):
-                if n > 0:
-                    pair = dws[2 * k : 2 * k + 2]
-                    bs = [dw_mm(n - 1, dd, gh) for dd, gh in pair]
-                    for (dd, gh), b in zip(pair, bs):
-                        dw_out(n - 1, dd, gh, b, "S")
-
-            for gh in range(2):
+        def step(s, n):
+            a = s.split(":")
+            k, e = a[0], a[1] if len(a) > 1 else "S"
+            m = n + 1 if "+" in k else (n - 1 if "-" in k else n)
+            if m < 0 or m >= BLOCKS:
+                return
+            k = k.replace("+", "").replace("-", "")
+            if (k, m) in done:
+                return
+            done.add((k, m))
+            g = 1 if k[-1] == "1" else 0
+            if k[:3] == "stt":
+                for j in range(4):
+                    stt(m, g, j, pend[m, g, j])
+            elif k[:2] == "dh":
+                for j in range(4):
+                    pend[m, g, j] = dh_mm(m, g, j)
+            elif k == "tg":
                 for h in range(2):
-                    bs = [dh_mm(n, gh, 2 * h + e) for e in range(2)]
-                    for e in range(2):
-                        stt(n, gh, 2 * h + e, bs[e])
-                    dw_pair(2 * gh + h)
-                if gh == 1:
-                    tr_dz(n, 0, 0, "S")
-                    tr_dz(n, 0, 1, "S")
-            t_di[n, 0] = interleave("dz_grp", t_d[n, 0], 2)
-            tr_dz(n, 1, 0, "S")
-            tr_dz(n, 1, 1, "S")
-            t_di[n, 1] = interleave("dz_grp", t_d[n, 1], 2)
-            q_dz[n, 0] = quantize(t_di[n, 0], E5M2, "dz", 4)
-            q_dzt[n, 0] = quantize(t_f[n, 0], E5M2, "dzt", 2)
-            q_dz[n, 1] = quantize(t_di[n, 1], E5M2, "dz", 4)
-            t_xi[n] = interleave("x_grp", t_x[n], 1)
-            q_dzt[n, 1] = quantize(t_f[n, 1], E5M2, "dzt", 2)
-            if n + 2 < BLOCKS:
-                load_w1(n + 2)
-                load_x(n + 2)
-            if n == 0:
-                for gh in range(2):
-                    tr_w1(0, gh, 0, "S")
-                    tr_w1(0, gh, 1, "S")
-            if not last:
-                tr_g(n + 1, 0, "S")
-                tr_g(n + 1, 1, "S")
-                for gh in range(2):
-                    tr_w2(n + 1, gh, 0, "S")
-                    tr_w2(n + 1, gh, 1, "S")
-            if n == 0:
-                for gh in range(2):
-                    q_w1[0, gh] = quantize(t_w1g[0, gh], E4M3, "w1", 4)
-            q_x[n] = quantize(t_xi[n], E4M3, "x", 2)
-            dxb = [dx_mm(n, j) for j in range(2)]
-            if not last:
-                q_g[n + 1] = quantize(t_gg[n + 1], E5M2, "g", 2)
-            for j in range(2):
-                dx_add(n, j, dxb[j])
-            dxb = [dx_mm(n, j) for j in range(2, 4)]
-            if not last:
-                for gh in range(2):
-                    q_w2[n + 1, gh] = quantize(t_w2g[n + 1, gh], E4M3, "w2", 4)
-            for j in range(2, 4):
-                dx_add(n, j, dxb[j - 2])
-            if not last:
-                for gh in range(2):
-                    tr_w1(n + 1, gh, 0, "S")
-                    tr_w1(n + 1, gh, 1, "S")
-                    exp(n + 1, gh)
-                for gh in range(2):
-                    q_w1[n + 1, gh] = quantize(t_w1g[n + 1, gh], E4M3, "w1", 4)
-        n = BLOCKS - 1
-        for gh in range(2):
-            for dd in range(4):
-                b = dw_mm(n, dd, gh)
-                dw_out(n, dd, gh, b, "S" if (dd + gh) % 2 == 0 else "V")
+                    tr_g(m, h, e[h % len(e)])
+            elif k[:3] == "tw2":
+                for h in range(2):
+                    tr_w2(m, g, h, e[h % len(e)])
+            elif k[:3] == "tw1":
+                for h in range(2):
+                    tr_w1(m, g, h, e[h % len(e)])
+            elif k[:3] == "tdz":
+                for h in range(2):
+                    tr_dz(m, g, h, e[h % len(e)])
+            elif k[:3] == "dxp":
+                for j in range(2 * g, 2 * g + 2):
+                    dx_add(m, j, dx_mm(m, j))
+            elif k[:3] == "dwp":
+                for i in range(4):
+                    dw_out(m, 2 * g + i // 2, i % 2, dw_mm(m, 2 * g + i // 2, i % 2), e[i % len(e)])
+            elif k[:3] == "dwg":
+                for i in range(4):
+                    dw_out(m, i, g, dw_mm(m, i, g), e[i % len(e)])
+            elif k[:2] == "di":
+                t_di[m, g] = interleave("dz_grp", t_d[m, g][:], 2, e)
+            elif k[:3] == "exp":
+                exp(m, g)
+            elif k == "qg":
+                q_g[m] = quantize(t_gg[m], E5M2, "g", 1)
+            elif k[:3] == "qw2":
+                q_w2[m, g] = quantize(t_w2g[m, g], E4M3, "w2", 2)
+            elif k[:4] == "qdzt":
+                q_dzt[m, g] = quantize(t_f[m, g], E5M2, "dzt", 2)
+            elif k[:3] == "qdz":
+                q_dz[m, g] = quantize(t_di[m, g], E5M2, "dz", 2)
+            elif k == "intx":
+                t_xi[m] = interleave("x_grp", t_x[m], 1, e)
+            elif k == "qx":
+                q_x[m] = quantize(t_xi[m], E4M3, "x", 1)
+            elif k[:3] == "qw1":
+                q_w1[m, g] = quantize(t_w1g[m, g], E4M3, "w1", 2)
+            elif k == "lg":
+                load_g(m)
+            elif k == "lw":
+                load_w2(m)
+            elif k == "lz":
+                load_z(m)
+            elif k == "lv":
+                load_w1(m)
+            elif k == "lx":
+                load_x(m)
+            else:
+                raise ValueError(k)
+
+        for n, s in PLAN:
+            for w in s.split():
+                step(w, n)

from contextlib import ExitStack

import concourse.mybir as mybir
from concourse.masks import make_identity

TOKENS, D_BLOCK, HID, BLOCKS = 512, 512, 1024, 4
FLOPS = 3 * 2 * BLOCKS * TOKENS * D_BLOCK * HID
BYTES = 2 * (2 * TOKENS * BLOCKS * D_BLOCK + 2 * BLOCKS * D_BLOCK * HID) + 4 * (
    BLOCKS * TOKENS * HID + TOKENS * BLOCKS * D_BLOCK + BLOCKS * D_BLOCK * HID
)

F32 = mybir.dt.float32
BF16 = mybir.dt.bfloat16
U32 = mybir.dt.uint32
U8 = mybir.dt.uint8
E4M3 = mybir.dt.float8_e4m3fn_x4
E5M2 = mybir.dt.float8_e5m2_x4
ACT = mybir.ActivationFunctionType
ALU = mybir.AluOpType

P = 128
N = 512
R = 4
BUFS = {"w1": 2, "z": 2, "E": 2, "grp": 7, "dz1": 2, "dx": 3, "dw": 6}
PLAN = [
    (0, "lg"),
    (0, "lw"),
    (0, "lz"),
    (0, "lv"),
    (1, "lw"),
    (0, "lx"),
    (1, "lg"),
    (1, "lz"),
    (2, "lw"),
    (1, "lv"),
    (3, "lw"),
    (2, "lz"),
    (3, "lv"),
    (1, "lx"),
    (3, "lz"),
    (2, "lv"),
    (0, "tg:SS qg tw20:VS exp0 qw20 tw21:VV qw21 exp1 dh0 dh1"),
    (0, "stt0 stt1 tdz0:SS tw11:SS tdz1:VS di1:s qdzt0 di0:G qdz0 qw11 qdzt1 tw10:SV qdz1 qw10 intx:V tw20+:SS tw21+:SS qx qw21+ dxp0 dwp0:SV dwp1:SV qw20+ tg+:SS qg+ dxp1 dh0+ exp0+ exp1+ dh1+"),
    (1, "intx:G tw20+:SS stt0 stt1 dxp1- tg+:VS di0:G tdz0:SV di1:V qw20+ qg+ tdz1:SS qdzt1 tw10:SS dwp0-:SSSSSV qdzt0 dxp0- tw11:SS dwp1-:SSSV tw21+:SS exp0+ qw10 qdz1 qdz0 exp1+ qw11 qw21+ dh0+ dh1+ qx"),
    (2, "intx:G tw20+:SS stt0 stt1 dxp1- tg+:VS di0:G tdz0:SV di1:V qw20+ qg+ tdz1:SS qdzt1 tw10:SS dwp0-:SSSSSV qdzt0 dxp0- tw11:SS dwp1-:SSSV tw21+:SS exp0+ qw10 qdz1 qdz0 exp1+ qw11 qw21+ dh0+ dh1+ qx"),
    (3, "tw11:SS stt0 stt1 dxp0- tw10:VS intx:G dwp1-:SV di0:G dwp0-:SSSV tdz1:SS di1:G tdz0:SS qdz0 qx dxp1- qdz1 qw11 qdzt0 qdzt1 qw10"),
    (4, "dwg0-:SSSV dwg1-:SSV dxp1- dxp0-"),
]


def tile_blockresmlp_mixerblock_pb_v_kernel(tc, x_blocks, w1, b1, w2, b2, z1, grad_out, out_0, out_1):
    nc = tc.nc

    g_view = grad_out.rearrange("(p j) c -> p j c", j=R)
    x_view = x_blocks.rearrange("(p j) c -> p j c", j=R)
    dx_view = out_0.rearrange("(p j) c -> p j c", j=R)

    with ExitStack() as ctx:
        const = ctx.enter_context(tc.tile_pool(name="const", bufs=1))
        raw = ctx.enter_context(tc.tile_pool(name="raw", bufs=2))
        work = ctx.enter_context(tc.tile_pool(name="work", bufs=2))
        codes = ctx.enter_context(tc.tile_pool(name="codes", bufs=2))
        outs = ctx.enter_context(tc.tile_pool(name="outs", bufs=3))
        psum = ctx.enter_context(tc.psum_pool(name="psum", bufs=8))

        ident = const.tile([P, P], F32, name="ident")
        make_identity(nc, ident[:])
        warm = const.tile([P, 1], F32, name="warm")
        nc.vector.memset(warm[:], 0.0)
        nc.scalar.activation(warm[:], warm[:], ACT.Exp)

        ctx.enter_context(tc.manual_schedule())

        t_g, t_x, t_w2, t_w1, t_z, t_e = {}, {}, {}, {}, {}, {}
        q_g, q_x, q_w2, q_w1, q_dz, q_dzt = {}, {}, {}, {}, {}, {}
        t_gg, t_xi, t_w2g, t_w1g, t_f, t_di, t_d = {}, {}, {}, {}, {}, {}, {}
        t_ow, t_dx = {}, {}
        done = set()

        def load_g(n):
            if n == 0:
                first = raw.tile([P, R, N], BF16, name="g_first", bufs=1)
                nc.sync.dma_start(out=first[:], in_=g_view[:, :, 0:N])
                t_g[0] = first[:]
            elif n == 1:
                rest = raw.tile([P, R, 3 * N], BF16, name="g_rest", bufs=1)
                nc.sync.dma_start(out=rest[:], in_=g_view[:, :, N : 4 * N])
                for m in range(1, 4):
                    t_g[m] = rest[:, :, (m - 1) * N : m * N]

        def load_x(n):
            if n > 0:
                return
            whole = raw.tile([P, R, BLOCKS * N], BF16, name="x_raw", bufs=1)
            nc.sync.dma_start(out=whole[:], in_=x_view)
            for m in range(BLOCKS):
                t_x[m] = whole[:, :, m * N : (m + 1) * N]

        def load_w2(n):
            t_w2[n] = raw.tile([P, 2, R, N], BF16, name="w2_raw", bufs=2)
            view = w2[n].rearrange("(g p r) d -> p g r d", g=2, r=R)
            for gh in range(2):
                nc.sync.dma_start(out=t_w2[n][:, gh], in_=view[:, gh])

        def load_w1(n):
            t_w1[n] = raw.tile([P, R, HID], BF16, name="w1_raw", bufs=BUFS["w1"])
            nc.sync.dma_start(out=t_w1[n][:], in_=w1[n].rearrange("(p r) h -> p r h", r=R))

        def load_z(n):
            t_z[n] = raw.tile([P, R, HID], F32, name="z_raw", bufs=BUFS["z"])
            view = z1[n].rearrange("(p j) h -> p j h", j=R)
            if n == 0:
                for k in range(2):
                    for jp in range(2):
                        js, hs = slice(2 * jp, 2 * jp + 2), slice(k * N, (k + 1) * N)
                        nc.sync.dma_start(out=t_z[n][:, js, hs], in_=view[:, js, hs])
            else:
                for jp in range(2):
                    js = slice(2 * jp, 2 * jp + 2)
                    nc.sync.dma_start(out=t_z[n][:, js, :], in_=view[:, js, :])

        def copy(engine, out, in_):
            if engine == "V":
                nc.vector.tensor_copy(out=out, in_=in_)
            else:
                nc.scalar.copy(out=out, in_=in_)

        def bank4(ins):
            bank = psum.tile([P, R, P], F32, name="bank")
            for k in range(R):
                nc.tensor.transpose(bank[:, k, :], ins[k], ident[:])
            return bank

        def rows_bank(ins, grouped, half, engine):
            copy(
                engine,
                grouped.bitcast(F32)[:, 2 * P * half : 2 * P * (half + 1), :].rearrange("q (e p) u -> q e p u", e=2),
                bank4(ins)[:].rearrange("q (e u) p -> q e p u", e=2),
            )

        def pairs_bank(ins, grouped, half, engine):
            copy(
                engine,
                grouped.bitcast(F32)[:, 2 * P * half : 2 * P * (half + 1), :].rearrange("q (p e) u -> q p (e u)", e=2),
                bank4(ins)[:].rearrange("q k p -> q p k"),
            )

        def quantize(grouped, dtype, name, bufs):
            c = codes.tile([P, N], U32, name=name + "_c", bufs=bufs, align_bytes=64)
            s = codes.tile([P, N], U8, name=name + "_s", bufs=bufs, align_bytes=64)
            nc.vector.quantize_mx(
                out=c[:].bitcast(dtype), scales=s[:], in_=grouped[:].rearrange("p c t -> p (c t)")
            )
            return c, s

        def mx(bank, a, a_type, a_cols, b, b_type, start, stop):
            nc.tensor.matmul_mx(
                out=bank[:],
                lhsT=a[0][:, a_cols].bitcast(a_type),
                lhsT_scale=a[1][:, a_cols],
                rhs=b[0][:].bitcast(b_type),
                rhs_scale=b[1][:],
                start=start,
                stop=stop,
            )

        def grouped_tile(name, bufs):
            return work.tile([P, N, R], BF16, name=name, bufs=bufs, align_bytes=64)

        def tr_g(n, jp, engine):
            if jp == 0:
                t_gg[n] = grouped_tile("grp", BUFS["grp"])
            words = t_g[n].bitcast(F32)
            rows_bank([words[:, 2 * jp + e, u::2] for e in range(2) for u in range(2)], t_gg[n][:], jp, engine)

        def tr_w2(n, gh, s, engine):
            if s == 0:
                t_w2g[n, gh] = grouped_tile("grp", BUFS["grp"])
            words = t_w2[n][:, gh].bitcast(F32)
            pairs_bank([words[:, 2 * s + e, u::2] for e in range(2) for u in range(2)], t_w2g[n, gh][:], s, engine)

        def tr_w1(n, gh, s, engine):
            if s == 0:
                t_w1g[n, gh] = grouped_tile("grp", BUFS["grp"])
            words = t_w1[n][:].bitcast(F32)
            pairs_bank(
                [words[:, 2 * s + e, 256 * gh + u : 256 * (gh + 1) : 2] for e in range(2) for u in range(2)],
                t_w1g[n, gh][:],
                s,
                engine,
            )

        def tr_dz(n, gh, jp, engine):
            if jp == 0:
                t_f[n, gh] = grouped_tile("grp", BUFS["grp"])
            words = t_d[n, gh][:].bitcast(F32)
            rows_bank(
                [words[:, 2 * jp + e, P * u : P * (u + 1)] for e in range(2) for u in range(2)],
                t_f[n, gh][:],
                jp,
                engine,
            )

        def interleave(name, src, bufs, engine):
            dst = grouped_tile(name, bufs)
            if engine == "G":
                nc.gpsimd.tensor_scalar(
                    out=dst[:],
                    in0=src.rearrange("p t c -> p c t"),
                    scalar1=1.0,
                    scalar2=0.0,
                    op0=ALU.mult,
                    op1=ALU.add,
                )
            elif engine == "s":
                nc.scalar.copy(
                    out=dst[:].rearrange("p (c i) t -> p c t i", i=4), in_=src.rearrange("p t (c i) -> p c t i", i=4)
                )
            else:
                nc.vector.tensor_copy(
                    out=dst[:].rearrange("p (c i) t -> p c t i", i=4), in_=src.rearrange("p t (c i) -> p c t i", i=4)
                )
            return dst

        def exp(n, gh):
            t_e[n, gh] = work.tile([P, R, N], F32, name="e", bufs=BUFS["E"])
            for j in range(R):
                nc.scalar.activation(
                    t_e[n, gh][:, j, :].rearrange("p (s i e) -> p s i e", s=2, e=2),
                    t_z[n][:, j, gh * N : (gh + 1) * N].rearrange("p (i s e) -> p s i e", s=2, e=2),
                    ACT.Exp,
                )

        def dh_mm(n, gh, j):
            bank = psum.tile([P, N], F32, name="bank")
            mx(bank, q_g[n], E5M2, slice(j * P, (j + 1) * P), q_w2[n, gh], E4M3, True, True)
            return bank

        def stt(n, gh, j, bank):
            if j == 0:
                t_d[n, gh] = work.tile([P, R, N], BF16, name="dz1", bufs=BUFS["dz1"], align_bytes=64)
            nc.vector.scalar_tensor_tensor(
                out=t_d[n, gh][:, j, :],
                in0=t_e[n, gh][:, j, :],
                scalar=1.0,
                in1=bank[:],
                op0=ALU.min,
                op1=ALU.mult,
            )

        def dx_mm(n, j):
            bank = psum.tile([P, N], F32, name="bank")
            for gh in range(2):
                mx(bank, q_dzt[n, gh], E5M2, slice(j * P, (j + 1) * P), q_w1[n, gh], E4M3, gh == 0, gh == 1)
            return bank

        def dx_add(n, j, bank):
            if j % 2 == 0:
                t_dx[n, j // 2] = outs.tile([P, 2, N], F32, name="dx", bufs=BUFS["dx"])
            t = t_dx[n, j // 2]
            nc.vector.tensor_tensor(
                out=t[:, j % 2, :].rearrange("p (i s e) -> p i s e", s=2, e=2),
                in0=bank[:].rearrange("p (s i e) -> p i s e", s=2, e=2),
                in1=t_g[n][:, j, :].rearrange("p (i s e) -> p i s e", s=2, e=2),
                op=ALU.add,
            )
            if j % 2 == 1:
                nc.sync.dma_start(out=dx_view[:, j - 1 : j + 1, n * N : (n + 1) * N], in_=t[:])

        def dw_mm(n, dd, gh):
            bank = psum.tile([P, N], F32, name="bank")
            mx(bank, q_x[n], E4M3, slice(dd * P, (dd + 1) * P), q_dz[n, gh], E5M2, True, True)
            return bank

        def dw_out(n, dd, gh, bank, engine):
            first = (n, dd) not in t_ow
            if first:
                t_ow[n, dd] = outs.tile([P, 2, N], F32, name="dw", bufs=BUFS["dw"])
            t = t_ow[n, dd]
            copy(
                engine,
                t[:, gh, :].rearrange("p (i s e) -> p i s e", s=2, e=2),
                bank[:].rearrange("p (s i e) -> p i s e", s=2, e=2),
            )
            if not first:
                nc.sync.dma_start(out=out_1[n, dd * P : (dd + 1) * P, :], in_=t[:].rearrange("p g h -> p (g h)"))

        pend = {}

        def step(s, n):
            a = s.split(":")
            k, e = a[0], a[1] if len(a) > 1 else "S"
            m = n + 1 if "+" in k else (n - 1 if "-" in k else n)
            if m < 0 or m >= BLOCKS:
                return
            k = k.replace("+", "").replace("-", "")
            if (k, m) in done:
                return
            done.add((k, m))
            g = 1 if k[-1] == "1" else 0
            if k[:3] == "stt":
                for j in range(4):
                    stt(m, g, j, pend[m, g, j])
            elif k[:2] == "dh":
                for j in range(4):
                    pend[m, g, j] = dh_mm(m, g, j)
            elif k == "tg":
                for h in range(2):
                    tr_g(m, h, e[h % len(e)])
            elif k[:3] == "tw2":
                for h in range(2):
                    tr_w2(m, g, h, e[h % len(e)])
            elif k[:3] == "tw1":
                for h in range(2):
                    tr_w1(m, g, h, e[h % len(e)])
            elif k[:3] == "tdz":
                for h in range(2):
                    tr_dz(m, g, h, e[h % len(e)])
            elif k[:3] == "dxp":
                for j in range(2 * g, 2 * g + 2):
                    dx_add(m, j, dx_mm(m, j))
            elif k[:3] == "dwp":
                for i in range(4):
                    dw_out(m, 2 * g + i // 2, i % 2, dw_mm(m, 2 * g + i // 2, i % 2), e[i % len(e)])
            elif k[:3] == "dwg":
                for i in range(4):
                    dw_out(m, i, g, dw_mm(m, i, g), e[i % len(e)])
            elif k[:2] == "di":
                t_di[m, g] = interleave("dz_grp", t_d[m, g][:], 2, e)
            elif k[:3] == "exp":
                exp(m, g)
            elif k == "qg":
                q_g[m] = quantize(t_gg[m], E5M2, "g", 1)
            elif k[:3] == "qw2":
                q_w2[m, g] = quantize(t_w2g[m, g], E4M3, "w2", 2)
            elif k[:4] == "qdzt":
                q_dzt[m, g] = quantize(t_f[m, g], E5M2, "dzt", 2)
            elif k[:3] == "qdz":
                q_dz[m, g] = quantize(t_di[m, g], E5M2, "dz", 2)
            elif k == "intx":
                t_xi[m] = interleave("x_grp", t_x[m], 1, e)
            elif k == "qx":
                q_x[m] = quantize(t_xi[m], E4M3, "x", 1)
            elif k[:3] == "qw1":
                q_w1[m, g] = quantize(t_w1g[m, g], E4M3, "w1", 2)
            elif k == "lg":
                load_g(m)
            elif k == "lw":
                load_w2(m)
            elif k == "lz":
                load_z(m)
            elif k == "lv":
                load_w1(m)
            elif k == "lx":
                load_x(m)
            else:
                raise ValueError(k)

        for n, s in PLAN:
            for w in s.split():
                step(w, n)
